import numpy as np
import ml_dtypes


def mxq(x, axis, fmt="e4m3"):
    dtype, down = {"e4m3": (ml_dtypes.float8_e4m3fn, 7), "e5m2": (ml_dtypes.float8_e5m2, 14)}[fmt]
    v = np.moveaxis(np.asarray(x, np.float32).astype(ml_dtypes.bfloat16).astype(np.float64), axis, -1)
    blocks = v.reshape(v.shape[:-1] + (-1, 32))
    amax = np.abs(blocks).max(-1, keepdims=True)
    byte = np.maximum(np.where(amax > 0, np.frexp(amax)[1] - 1 + 127, 0) - down, 1)
    scale = np.exp2(byte - 127.0)
    codes = (blocks / scale).astype(np.float32).astype(dtype).astype(np.float64)
    return np.moveaxis((codes * scale).reshape(v.shape), -1, axis)


WIDE = False


def mx_kscale(k):
    if not WIDE:
        return np.ones(k)
    levels = np.array([10, -10, 5, -5, 0])
    a = np.random.permutation(np.resize(levels, k // 512 * 4)).reshape(k // 512, 4)
    idx = np.arange(k)
    return np.exp2(a[idx // 512, idx % 128 // 32])


BF16 = ml_dtypes.bfloat16


def bf(x):
    return np.asarray(x, np.float32).astype(BF16)


def f64(x):
    return np.asarray(x).astype(np.float64)


B, DA, DB, DC, OUT, NS = 4096, 512, 512, 1024, 128, 3
EPS = 1e-5
STREAMS = (("a", DA), ("b", DB), ("c", DC))


def layer_norm(x, w, b):
    mu = x.mean(-1, keepdims=True)
    var = np.square(x - mu).mean(-1, keepdims=True)
    return (x - mu) / np.sqrt(var + EPS) * w + b


def setup_inputs():
    inp = {}
    for name, d in STREAMS:
        t = mx_kscale(d)
        loud = np.exp2(-np.random.uniform(0.0, 8.0, (B, 1)))
        inp["x_" + name] = bf((np.random.standard_normal((B, d)) + 0.5 * np.random.standard_normal((B, 1))) * loud)
        inp["ln_w_" + name] = bf((1.0 + 0.1 * np.random.standard_normal(d)) * t)
        inp["ln_b_" + name] = bf(0.1 * np.random.standard_normal(d) * t)
        inp["W_" + name] = bf(np.random.standard_normal((d, OUT)) / np.sqrt(d) / t[:, None])
        inp["b_" + name] = bf(0.2 * np.random.standard_normal(OUT))
        inp["Wg_" + name] = bf(np.random.standard_normal((d, NS * OUT)) / np.sqrt(d) / t[:, None])
        inp["bg_" + name] = bf(0.2 * np.random.standard_normal(NS * OUT))
    return inp


def reference(x_a, ln_w_a, ln_b_a, W_a, b_a, Wg_a, bg_a,
              x_b, ln_w_b, ln_b_b, W_b, b_b, Wg_b, bg_b,
              x_c, ln_w_c, ln_b_c, W_c, b_c, Wg_c, bg_c):
    streams = ((x_a, ln_w_a, ln_b_a, W_a, b_a, Wg_a, bg_a),
               (x_b, ln_w_b, ln_b_b, W_b, b_b, Wg_b, bg_b),
               (x_c, ln_w_c, ln_b_c, W_c, b_c, Wg_c, bg_c))
    gate_logits = 0.0
    outputs = []
    for x, lw, lb, W, b, Wg, bg in streams:
        f = np.maximum(layer_norm(f64(x), f64(lw), f64(lb)), 0.0)
        fq = mxq(f, 1, "e4m3")
        outputs.append((fq @ mxq(f64(W), 0, "e4m3")) + f64(b))
        gate_logits = gate_logits + ((fq @ mxq(f64(Wg), 0, "e4m3")) + f64(bg))
    g = gate_logits.reshape(B, NS, OUT)
    e = np.exp(g - g.max(1, keepdims=True))
    gate = e / e.sum(1, keepdims=True)
    return sum(gate[:, i] * outputs[i] for i in range(NS))

@@ -1,0 +1,291 @@
+from contextlib import ExitStack
+
+import concourse.mybir as mybir
+from concourse.masks import make_identity
+
+F32 = mybir.dt.float32
+BF16 = mybir.dt.bfloat16
+U32 = mybir.dt.uint32
+U8 = mybir.dt.uint8
+FP8X4 = mybir.dt.float8_e4m3fn_x4
+ALU = mybir.AluOpType
+ACT = mybir.ActivationFunctionType
+
+P = 128
+PACK = 4
+K_PASS = P * PACK
+ROWS = 4096
+BLOCK = 512
+ROW_TILES = BLOCK // P
+N_BLOCKS = ROWS // BLOCK
+OUT = 128
+NS = 3
+K_ALL = 2048
+PASSES = K_ALL // K_PASS
+STREAM_OF_PASS = (0, 1, 2, 2)
+PASSES_OF_STREAM = ((0,), (1,), (2, 3))
+W_COLS = OUT + NS * OUT
+EPS = 1e-5
+
+LN_W_ROW = 0
+LN_B_ROW = K_ALL // P
+OUT_BIAS_ROW = 2 * (K_ALL // P)
+GATE_BIAS_ROW = OUT_BIAS_ROW + NS
+PARAM_ROWS = GATE_BIAS_ROW + NS * NS
+
+FLOPS = 2 * ROWS * K_ALL * W_COLS
+
+
+def regroup(nc, grouped, planes):
+    nc.vector.tensor_copy(
+        out=grouped.rearrange("p (c i) t -> p c t i", i=4),
+        in_=planes.rearrange("p t (c i) -> p c t i", i=4),
+    )
+
+
+def tile_vectormerge_pa_t_kernel(
+    tc,
+    x_a, ln_w_a, ln_b_a, W_a, b_a, Wg_a, bg_a,
+    x_b, ln_w_b, ln_b_b, W_b, b_b, Wg_b, bg_b,
+    x_c, ln_w_c, ln_b_c, W_c, b_c, Wg_c, bg_c,
+    out,
+):
+    nc = tc.nc
+    xs = (x_a, x_b, x_c)
+    ln_ws = (ln_w_a, ln_w_b, ln_w_c)
+    ln_bs = (ln_b_a, ln_b_b, ln_b_c)
+    Ws = (W_a, W_b, W_c)
+    bs = (b_a, b_b, b_c)
+    Wgs = (Wg_a, Wg_b, Wg_c)
+    bgs = (bg_a, bg_b, bg_c)
+
+    with ExitStack() as ctx:
+        keep = ctx.enter_context(tc.tile_pool(name="keep", bufs=1))
+        x_pool = ctx.enter_context(tc.tile_pool(name="x_pool", bufs=3))
+        stat_pool = ctx.enter_context(tc.tile_pool(name="stat_pool", bufs=3))
+        norm_pool = ctx.enter_context(tc.tile_pool(name="norm_pool", bufs=3))
+        f_pool = ctx.enter_context(tc.tile_pool(name="f_pool", bufs=2))
+        code_pool = ctx.enter_context(tc.tile_pool(name="code_pool", bufs=2))
+        gate_pool = ctx.enter_context(tc.tile_pool(name="gate_pool", bufs=2))
+        psum_xt = ctx.enter_context(tc.psum_pool(name="psum_xt", bufs=3))
+        psum_mx = ctx.enter_context(tc.psum_pool(name="psum_mx", bufs=1))
+        psum_sn = ctx.enter_context(tc.psum_pool(name="psum_sn", bufs=1))
+
+        ident_f32 = keep.tile([P, P], F32)
+        make_identity(nc, ident_f32[:])
+        ident_bf16 = keep.tile([P, P], BF16)
+        make_identity(nc, ident_bf16[:])
+        minus_half = keep.tile([P, ROW_TILES, NS], F32)
+        nc.vector.memset(minus_half[:], -0.5)
+
+        param_rows = keep.tile([P, P], BF16)
+        nc.vector.memset(param_rows[:], 0.0)
+        for s in range(NS):
+            first = PASSES_OF_STREAM[s][0] * PACK
+            chunks = len(PASSES_OF_STREAM[s]) * PACK
+            nc.sync.dma_start(
+                out=param_rows[LN_W_ROW + first : LN_W_ROW + first + chunks, :],
+                in_=ln_ws[s].rearrange("(c p) -> c p", p=P),
+            )
+            nc.sync.dma_start(
+                out=param_rows[LN_B_ROW + first : LN_B_ROW + first + chunks, :],
+                in_=ln_bs[s].rearrange("(c p) -> c p", p=P),
+            )
+            nc.sync.dma_start(
+                out=param_rows[OUT_BIAS_ROW + s : OUT_BIAS_ROW + s + 1, :],
+                in_=bs[s].rearrange("(c p) -> c p", p=P),
+            )
+            nc.sync.dma_start(
+                out=param_rows[GATE_BIAS_ROW + NS * s : GATE_BIAS_ROW + NS * (s + 1), :],
+                in_=bgs[s].rearrange("(c p) -> c p", p=P),
+            )
+        param_ps = psum_xt.tile([P, P], BF16, tag="xt")
+        nc.tensor.transpose(param_ps[:], param_rows[:], ident_bf16[:])
+        param = keep.tile([P, P], F32)
+        nc.vector.tensor_copy(out=param[:], in_=param_ps[:])
+        gate_bias = keep.tile([P, NS], F32)
+        nc.vector.tensor_add(
+            out=gate_bias[:],
+            in0=param[:, GATE_BIAS_ROW : GATE_BIAS_ROW + NS],
+            in1=param[:, GATE_BIAS_ROW + NS : GATE_BIAS_ROW + 2 * NS],
+        )
+        nc.vector.tensor_add(
+            out=gate_bias[:],
+            in0=gate_bias[:],
+            in1=param[:, GATE_BIAS_ROW + 2 * NS : GATE_BIAS_ROW + 3 * NS],
+        )
+
+        w_raw = keep.tile([P, PASSES, PACK, W_COLS], BF16)
+        for s in range(NS):
+            g0 = PASSES_OF_STREAM[s][0]
+            g1 = PASSES_OF_STREAM[s][-1] + 1
+            rows_view = w_raw[:, g0:g1, :, :].rearrange("p g t n -> p (g t) n")
+            nc.sync.dma_start(
+                out=rows_view[:, :, 0:OUT], in_=Ws[s].rearrange("(c p) n -> p c n", p=P)
+            )
+            nc.sync.dma_start(
+                out=rows_view[:, :, OUT:W_COLS], in_=Wgs[s].rearrange("(c p) n -> p c n", p=P)
+            )
+        w_grouped = keep.tile([P, PASSES, W_COLS, PACK], BF16, align_bytes=64)
+        w_codes = keep.tile([P, PASSES, W_COLS], U32, align_bytes=64)
+        w_scales = keep.tile([P, PASSES, W_COLS], U8, align_bytes=64)
+        for g in range(PASSES):
+            regroup(nc, w_grouped[:, g, :, :], w_raw[:, g, :, :])
+        for g in range(PASSES):
+            nc.vector.quantize_mx(
+                out=w_codes[:, g, :].bitcast(FP8X4),
+                scales=w_scales[:, g, :],
+                in_=w_grouped[:, g, :, :].rearrange("p n t -> p (n t)"),
+            )
+
+
+        def load(b):
+            x_blk = x_pool.tile([P, ROW_TILES, K_ALL], BF16)
+            rows = slice(b * BLOCK, (b + 1) * BLOCK)
+            for s in range(NS):
+                k0 = PASSES_OF_STREAM[s][0] * K_PASS
+                k1 = (PASSES_OF_STREAM[s][-1] + 1) * K_PASS
+                nc.sync.dma_start(
+                    out=x_blk[:, :, k0:k1],
+                    in_=xs[s][rows, :].rearrange("(p t) k -> p t k", t=ROW_TILES),
+                )
+            return x_blk
+
+        def statistics(x_blk):
+            partial = stat_pool.tile([P, ROW_TILES, PASSES, 6], F32)
+            mean_var = stat_pool.tile([P, ROW_TILES, NS, 2], F32)
+            for t in range(ROW_TILES):
+                for g in range(PASSES):
+                    nc.vector.bn_stats(
+                        out=partial[:, t, g, :], in_=x_blk[:, t, g * K_PASS : (g + 1) * K_PASS]
+                    )
+                for s in range(NS):
+                    g0 = PASSES_OF_STREAM[s][0]
+                    g1 = PASSES_OF_STREAM[s][-1] + 1
+                    nc.vector.bn_aggr(
+                        out=mean_var[:, t, s, :],
+                        in_=partial[:, t, g0:g1, :].rearrange("p g v -> p (g v)"),
+                    )
+            var_eps = stat_pool.tile([P, ROW_TILES, NS], F32)
+            nc.vector.tensor_scalar_add(out=var_eps[:], in0=mean_var[:, :, :, 1], scalar1=EPS)
+            rstd = stat_pool.tile([P, ROW_TILES, NS], F32)
+            nc.gpsimd.tensor_tensor(out=rstd[:], in0=var_eps[:], in1=minus_half[:], op=ALU.pow)
+            shift = stat_pool.tile([P, ROW_TILES, NS], F32)
+            nc.vector.scalar_tensor_tensor(
+                out=shift[:], in0=mean_var[:, :, :, 0], scalar=-1.0, in1=rstd[:],
+                op0=ALU.mult, op1=ALU.mult,
+            )
+            return rstd, shift
+
+        def features(x_blk, rstd, shift, f_codes, f_scales, g):
+            s = STREAM_OF_PASS[g]
+            x_norm = norm_pool.tile([P, ROW_TILES, K_PASS], F32)
+            for t in range(ROW_TILES):
+                nc.scalar.activation(
+                    out=x_norm[:, t, :], in_=x_blk[:, t, g * K_PASS : (g + 1) * K_PASS],
+                    func=ACT.Identity, scale=rstd[:, t, s : s + 1], bias=shift[:, t, s : s + 1],
+                )
+            planes = f_pool.tile([P, PACK, BLOCK], BF16)
+            for j in range(PACK):
+                chunk = g * PACK + j
+                x_t = psum_xt.tile([P, BLOCK], F32, tag="xt")
+                for t in range(ROW_TILES):
+                    nc.tensor.transpose(
+                        x_t[:, t * P : (t + 1) * P], x_norm[:, t, j * P : (j + 1) * P], ident_f32[:]
+                    )
+                nc.scalar.activation(
+                    out=planes[:, j, :], in_=x_t[:], func=ACT.Relu,
+                    scale=param[:, LN_W_ROW + chunk : LN_W_ROW + chunk + 1],
+                    bias=param[:, LN_B_ROW + chunk : LN_B_ROW + chunk + 1],
+                )
+            grouped = f_pool.tile([P, BLOCK, PACK], BF16, align_bytes=64)
+            regroup(nc, grouped[:], planes[:])
+            nc.vector.quantize_mx(
+                out=f_codes[:, g, :].bitcast(FP8X4),
+                scales=f_scales[:, g, :],
+                in_=grouped[:].rearrange("p r t -> p (r t)"),
+            )
+
+        def product(acc, f_codes, f_scales, passes, first_col):
+            cols = slice(first_col, first_col + P)
+            for g in passes:
+                nc.tensor.matmul_mx(
+                    out=acc[:],
+                    lhsT=w_codes[:, g, cols].bitcast(FP8X4), lhsT_scale=w_scales[:, g, cols],
+                    rhs=f_codes[:, g, :].bitcast(FP8X4), rhs_scale=f_scales[:, g, :],
+                    start=(g == passes[0]), stop=(g == passes[-1]),
+                )
+
+        def sum_transposed(acc, terms):
+            for t in range(ROW_TILES):
+                for i in range(NS):
+                    nc.tensor.matmul(
+                        out=acc[:, t * P : (t + 1) * P], lhsT=terms[i][:, t * P : (t + 1) * P],
+                        rhs=ident_f32[:], is_transpose=True, start=(i == 0), stop=(i == NS - 1),
+                    )
+
+        def merge(b, f_codes, f_scales):
+            all_passes = tuple(range(PASSES))
+            logits = []
+            for i in range(NS):
+                logit = psum_mx.tile([P, BLOCK], F32, name="logit%d" % i, tag="mx%d" % i)
+                product(logit, f_codes, f_scales, all_passes, OUT + i * OUT)
+                logits.append(logit)
+            biased0 = gate_pool.tile([P, BLOCK], F32)
+            nc.scalar.activation(
+                out=biased0[:], in_=logits[0][:], func=ACT.Identity, bias=gate_bias[:, 0:1], scale=1.0
+            )
+            top01 = gate_pool.tile([P, BLOCK], F32)
+            nc.vector.scalar_tensor_tensor(
+                out=top01[:], in0=logits[1][:], scalar=gate_bias[:, 1:2], in1=biased0[:],
+                op0=ALU.add, op1=ALU.max,
+            )
+            top = gate_pool.tile([P, BLOCK], F32)
+            nc.vector.scalar_tensor_tensor(
+                out=top[:], in0=logits[2][:], scalar=gate_bias[:, 2:3], in1=top01[:],
+                op0=ALU.add, op1=ALU.max,
+            )
+            expo = []
+            for i in range(NS):
+                below = gate_pool.tile([P, BLOCK], F32, name="below%d" % i)
+                if i == 0:
+                    nc.vector.tensor_sub(out=below[:], in0=biased0[:], in1=top[:])
+                else:
+                    nc.vector.scalar_tensor_tensor(
+                        out=below[:], in0=logits[i][:], scalar=gate_bias[:, i : i + 1], in1=top[:],
+                        op0=ALU.add, op1=ALU.subtract,
+                    )
+                e = gate_pool.tile([P, BLOCK], F32, name="expo%d" % i)
+                nc.scalar.activation(out=e[:], in_=below[:], func=ACT.Exp)
+                expo.append(e)
+            weighted = []
+            for s in range(NS):
+                y = psum_mx.tile([P, BLOCK], F32, name="y%d" % s, tag="mx%d" % s)
+                product(y, f_codes, f_scales, PASSES_OF_STREAM[s], 0)
+                w = gate_pool.tile([P, BLOCK], F32, name="weighted%d" % s)
+                nc.vector.scalar_tensor_tensor(
+                    out=w[:], in0=y[:], scalar=param[:, OUT_BIAS_ROW + s : OUT_BIAS_ROW + s + 1],
+                    in1=expo[s][:], op0=ALU.add, op1=ALU.mult,
+                )
+                weighted.append(w)
+            denom = psum_sn.tile([P, BLOCK], F32)
+            sum_transposed(denom, expo)
+            numer = psum_sn.tile([P, BLOCK], F32)
+            sum_transposed(numer, weighted)
+            inverse = gate_pool.tile([P, BLOCK], F32)
+            nc.vector.reciprocal(out=inverse[:], in_=denom[:])
+            merged = gate_pool.tile([P, BLOCK], F32)
+            nc.vector.tensor_mul(out=merged[:], in0=numer[:], in1=inverse[:])
+            nc.sync.dma_start(
+                out=out[b * BLOCK : (b + 1) * BLOCK, :].rearrange("(p t) n -> p (t n)", t=ROW_TILES),
+                in_=merged[:],
+            )
+
+        for b in range(N_BLOCKS):
+            x_blk = load(b)
+            rstd, shift = statistics(x_blk)
+            f_codes = code_pool.tile([P, PASSES, BLOCK], U32, align_bytes=64)
+            f_scales = code_pool.tile([P, PASSES, BLOCK], U8, align_bytes=64)
+            for g in range(PASSES):
+                features(x_blk, rstd, shift, f_codes, f_scales, g)
+            merge(b, f_codes, f_scales)

@@ -35,6 +35,14 @@ PARAM_ROWS = GATE_BIAS_ROW + NS * NS
 
 FLOPS = 2 * ROWS * K_ALL * W_COLS
 
+STEPS_PER_BLOCK = PASSES
+NORM_LAG = 5
+TRANSPOSE_LAG = NORM_LAG + 1
+REGROUP_LAG = TRANSPOSE_LAG + 1
+QUANT_LAG = REGROUP_LAG + 1
+MERGE_LAG = QUANT_LAG + STEPS_PER_BLOCK
+N_STEPS = N_BLOCKS * STEPS_PER_BLOCK + MERGE_LAG
+
 
 def regroup(nc, grouped, planes):
     nc.vector.tensor_copy(
@@ -61,15 +69,18 @@ def tile_vectormerge_pa_t_kernel(
 
     with ExitStack() as ctx:
         keep = ctx.enter_context(tc.tile_pool(name="keep", bufs=1))
-        x_pool = ctx.enter_context(tc.tile_pool(name="x_pool", bufs=3))
+        x_pool = ctx.enter_context(tc.tile_pool(name="x_pool", bufs=4))
         stat_pool = ctx.enter_context(tc.tile_pool(name="stat_pool", bufs=3))
         norm_pool = ctx.enter_context(tc.tile_pool(name="norm_pool", bufs=3))
         f_pool = ctx.enter_context(tc.tile_pool(name="f_pool", bufs=2))
         code_pool = ctx.enter_context(tc.tile_pool(name="code_pool", bufs=2))
-        gate_pool = ctx.enter_context(tc.tile_pool(name="gate_pool", bufs=2))
+        gate_pool = ctx.enter_context(tc.tile_pool(name="gate_pool", bufs=1))
+        out_pool = ctx.enter_context(tc.tile_pool(name="out_pool", bufs=2))
         psum_xt = ctx.enter_context(tc.psum_pool(name="psum_xt", bufs=3))
         psum_mx = ctx.enter_context(tc.psum_pool(name="psum_mx", bufs=1))
         psum_sn = ctx.enter_context(tc.psum_pool(name="psum_sn", bufs=1))
+
+        ctx.enter_context(tc.manual_schedule())
 
         ident_f32 = keep.tile([P, P], F32)
         make_identity(nc, ident_f32[:])
@@ -77,142 +88,165 @@ def tile_vectormerge_pa_t_kernel(
         make_identity(nc, ident_bf16[:])
         minus_half = keep.tile([P, ROW_TILES, NS], F32)
         nc.vector.memset(minus_half[:], -0.5)
-
         param_rows = keep.tile([P, P], BF16)
         nc.vector.memset(param_rows[:], 0.0)
-        for s in range(NS):
-            first = PASSES_OF_STREAM[s][0] * PACK
-            chunks = len(PASSES_OF_STREAM[s]) * PACK
-            nc.sync.dma_start(
-                out=param_rows[LN_W_ROW + first : LN_W_ROW + first + chunks, :],
-                in_=ln_ws[s].rearrange("(c p) -> c p", p=P),
-            )
-            nc.sync.dma_start(
-                out=param_rows[LN_B_ROW + first : LN_B_ROW + first + chunks, :],
-                in_=ln_bs[s].rearrange("(c p) -> c p", p=P),
-            )
-            nc.sync.dma_start(
-                out=param_rows[OUT_BIAS_ROW + s : OUT_BIAS_ROW + s + 1, :],
-                in_=bs[s].rearrange("(c p) -> c p", p=P),
-            )
-            nc.sync.dma_start(
-                out=param_rows[GATE_BIAS_ROW + NS * s : GATE_BIAS_ROW + NS * (s + 1), :],
-                in_=bgs[s].rearrange("(c p) -> c p", p=P),
-            )
-        param_ps = psum_xt.tile([P, P], BF16, tag="xt")
-        nc.tensor.transpose(param_ps[:], param_rows[:], ident_bf16[:])
         param = keep.tile([P, P], F32)
-        nc.vector.tensor_copy(out=param[:], in_=param_ps[:])
         gate_bias = keep.tile([P, NS], F32)
-        nc.vector.tensor_add(
-            out=gate_bias[:],
-            in0=param[:, GATE_BIAS_ROW : GATE_BIAS_ROW + NS],
-            in1=param[:, GATE_BIAS_ROW + NS : GATE_BIAS_ROW + 2 * NS],
-        )
-        nc.vector.tensor_add(
-            out=gate_bias[:],
-            in0=gate_bias[:],
-            in1=param[:, GATE_BIAS_ROW + 2 * NS : GATE_BIAS_ROW + 3 * NS],
-        )
-
         w_raw = keep.tile([P, PASSES, PACK, W_COLS], BF16)
-        for s in range(NS):
-            g0 = PASSES_OF_STREAM[s][0]
-            g1 = PASSES_OF_STREAM[s][-1] + 1
-            rows_view = w_raw[:, g0:g1, :, :].rearrange("p g t n -> p (g t) n")
-            nc.sync.dma_start(
-                out=rows_view[:, :, 0:OUT], in_=Ws[s].rearrange("(c p) n -> p c n", p=P)
-            )
-            nc.sync.dma_start(
-                out=rows_view[:, :, OUT:W_COLS], in_=Wgs[s].rearrange("(c p) n -> p c n", p=P)
-            )
         w_grouped = keep.tile([P, PASSES, W_COLS, PACK], BF16, align_bytes=64)
         w_codes = keep.tile([P, PASSES, W_COLS], U32, align_bytes=64)
         w_scales = keep.tile([P, PASSES, W_COLS], U8, align_bytes=64)
-        for g in range(PASSES):
-            regroup(nc, w_grouped[:, g, :, :], w_raw[:, g, :, :])
-        for g in range(PASSES):
-            nc.vector.quantize_mx(
-                out=w_codes[:, g, :].bitcast(FP8X4),
-                scales=w_scales[:, g, :],
-                in_=w_grouped[:, g, :, :].rearrange("p n t -> p (n t)"),
+
+        def load_small_vectors():
+            for s in range(NS):
+                first = PASSES_OF_STREAM[s][0] * PACK
+                chunks = len(PASSES_OF_STREAM[s]) * PACK
+                nc.sync.dma_start(
+                    out=param_rows[LN_W_ROW + first : LN_W_ROW + first + chunks, :],
+                    in_=ln_ws[s].rearrange("(c p) -> c p", p=P),
+                )
+                nc.sync.dma_start(
+                    out=param_rows[LN_B_ROW + first : LN_B_ROW + first + chunks, :],
+                    in_=ln_bs[s].rearrange("(c p) -> c p", p=P),
+                )
+                nc.sync.dma_start(
+                    out=param_rows[OUT_BIAS_ROW + s : OUT_BIAS_ROW + s + 1, :],
+                    in_=bs[s].rearrange("(c p) -> c p", p=P),
+                )
+                nc.sync.dma_start(
+                    out=param_rows[GATE_BIAS_ROW + NS * s : GATE_BIAS_ROW + NS * (s + 1), :],
+                    in_=bgs[s].rearrange("(c p) -> c p", p=P),
+                )
+            param_ps = psum_xt.tile([P, P], BF16, tag="xt")
+            nc.tensor.transpose(param_ps[:], param_rows[:], ident_bf16[:])
+            nc.scalar.copy(out=param[:], in_=param_ps[:])
+            nc.gpsimd.tensor_add(
+                out=gate_bias[:],
+                in0=param[:, GATE_BIAS_ROW : GATE_BIAS_ROW + NS],
+                in1=param[:, GATE_BIAS_ROW + NS : GATE_BIAS_ROW + 2 * NS],
+            )
+            nc.gpsimd.tensor_add(
+                out=gate_bias[:],
+                in0=gate_bias[:],
+                in1=param[:, GATE_BIAS_ROW + 2 * NS : GATE_BIAS_ROW + 3 * NS],
             )
 
+        def load_weights():
+            for s in range(NS):
+                g0 = PASSES_OF_STREAM[s][0]
+                g1 = PASSES_OF_STREAM[s][-1] + 1
+                rows_view = w_raw[:, g0:g1, :, :].rearrange("p g t n -> p (g t) n")
+                nc.sync.dma_start(
+                    out=rows_view[:, :, 0:OUT], in_=Ws[s].rearrange("(c p) n -> p c n", p=P)
+                )
+                nc.sync.dma_start(
+                    out=rows_view[:, :, OUT:W_COLS], in_=Wgs[s].rearrange("(c p) n -> p c n", p=P)
+                )
+
+        def quantise_weights():
+            for g in range(PASSES):
+                regroup(nc, w_grouped[:, g, :, :], w_raw[:, g, :, :])
+            for g in range(PASSES):
+                nc.vector.quantize_mx(
+                    out=w_codes[:, g, :].bitcast(FP8X4),
+                    scales=w_scales[:, g, :],
+                    in_=w_grouped[:, g, :, :].rearrange("p n t -> p (n t)"),
+                )
+
+        x_blks = {}
+        partials = {}
+        neg_means = {}
+        rstds = {}
+        x_norms = {}
+        planes_of = {}
+        grouped_of = {}
+        f_codes_of = {}
+        f_scales_of = {}
+        gate = {}
 
         def load(b):
-            x_blk = x_pool.tile([P, ROW_TILES, K_ALL], BF16)
+            x_blks[b] = x_pool.tile([P, ROW_TILES, K_ALL], BF16, name="x_blk")
             rows = slice(b * BLOCK, (b + 1) * BLOCK)
             for s in range(NS):
                 k0 = PASSES_OF_STREAM[s][0] * K_PASS
                 k1 = (PASSES_OF_STREAM[s][-1] + 1) * K_PASS
                 nc.sync.dma_start(
-                    out=x_blk[:, :, k0:k1],
+                    out=x_blks[b][:, :, k0:k1],
                     in_=xs[s][rows, :].rearrange("(p t) k -> p t k", t=ROW_TILES),
                 )
-            return x_blk
 
-        def statistics(x_blk):
-            partial = stat_pool.tile([P, ROW_TILES, PASSES, 6], F32)
+        def statistics(b, g):
+            if g == 0:
+                partials[b] = stat_pool.tile([P, ROW_TILES, PASSES, 6], F32, name="partial")
+            for t in range(ROW_TILES):
+                nc.vector.bn_stats(
+                    out=partials[b][:, t, g, :], in_=x_blks[b][:, t, g * K_PASS : (g + 1) * K_PASS]
+                )
+
+        def row_scalars(b):
             mean_var = stat_pool.tile([P, ROW_TILES, NS, 2], F32)
             for t in range(ROW_TILES):
-                for g in range(PASSES):
-                    nc.vector.bn_stats(
-                        out=partial[:, t, g, :], in_=x_blk[:, t, g * K_PASS : (g + 1) * K_PASS]
-                    )
                 for s in range(NS):
                     g0 = PASSES_OF_STREAM[s][0]
                     g1 = PASSES_OF_STREAM[s][-1] + 1
                     nc.vector.bn_aggr(
                         out=mean_var[:, t, s, :],
-                        in_=partial[:, t, g0:g1, :].rearrange("p g v -> p (g v)"),
+                        in_=partials[b][:, t, g0:g1, :].rearrange("p g v -> p (g v)"),
                     )
             var_eps = stat_pool.tile([P, ROW_TILES, NS], F32)
             nc.vector.tensor_scalar_add(out=var_eps[:], in0=mean_var[:, :, :, 1], scalar1=EPS)
-            rstd = stat_pool.tile([P, ROW_TILES, NS], F32)
-            nc.gpsimd.tensor_tensor(out=rstd[:], in0=var_eps[:], in1=minus_half[:], op=ALU.pow)
-            shift = stat_pool.tile([P, ROW_TILES, NS], F32)
-            nc.vector.scalar_tensor_tensor(
-                out=shift[:], in0=mean_var[:, :, :, 0], scalar=-1.0, in1=rstd[:],
-                op0=ALU.mult, op1=ALU.mult,
-            )
-            return rstd, shift
+            neg_means[b] = stat_pool.tile([P, ROW_TILES, NS], F32, name="neg_mean")
+            nc.vector.tensor_scalar_mul(out=neg_means[b][:], in0=mean_var[:, :, :, 0], scalar1=-1.0)
+            rstds[b] = stat_pool.tile([P, ROW_TILES, NS], F32, name="rstd")
+            nc.gpsimd.tensor_tensor(out=rstds[b][:], in0=var_eps[:], in1=minus_half[:], op=ALU.pow)
 
-        def features(x_blk, rstd, shift, f_codes, f_scales, g):
+        def normalise(b, g):
             s = STREAM_OF_PASS[g]
-            x_norm = norm_pool.tile([P, ROW_TILES, K_PASS], F32)
+            x_norms[b, g] = norm_pool.tile([P, ROW_TILES, K_PASS], F32, name="x_norm")
             for t in range(ROW_TILES):
-                nc.scalar.activation(
-                    out=x_norm[:, t, :], in_=x_blk[:, t, g * K_PASS : (g + 1) * K_PASS],
-                    func=ACT.Identity, scale=rstd[:, t, s : s + 1], bias=shift[:, t, s : s + 1],
+                nc.gpsimd.tensor_scalar(
+                    out=x_norms[b, g][:, t, :], in0=x_blks[b][:, t, g * K_PASS : (g + 1) * K_PASS],
+                    scalar1=neg_means[b][:, t, s : s + 1], scalar2=rstds[b][:, t, s : s + 1],
+                    op0=ALU.add, op1=ALU.mult,
                 )
-            planes = f_pool.tile([P, PACK, BLOCK], BF16)
+
+        def transpose_and_scale(b, g):
+            planes_of[b, g] = f_pool.tile([P, PACK, BLOCK], BF16, name="planes")
             for j in range(PACK):
                 chunk = g * PACK + j
                 x_t = psum_xt.tile([P, BLOCK], F32, tag="xt")
                 for t in range(ROW_TILES):
                     nc.tensor.transpose(
-                        x_t[:, t * P : (t + 1) * P], x_norm[:, t, j * P : (j + 1) * P], ident_f32[:]
+                        x_t[:, t * P : (t + 1) * P], x_norms[b, g][:, t, j * P : (j + 1) * P],
+                        ident_f32[:],
                     )
                 nc.scalar.activation(
-                    out=planes[:, j, :], in_=x_t[:], func=ACT.Relu,
+                    out=planes_of[b, g][:, j, :], in_=x_t[:], func=ACT.Relu,
                     scale=param[:, LN_W_ROW + chunk : LN_W_ROW + chunk + 1],
                     bias=param[:, LN_B_ROW + chunk : LN_B_ROW + chunk + 1],
                 )
-            grouped = f_pool.tile([P, BLOCK, PACK], BF16, align_bytes=64)
-            regroup(nc, grouped[:], planes[:])
+
+        def regroup_features(b, g):
+            grouped_of[b, g] = f_pool.tile([P, BLOCK, PACK], BF16, name="grouped", align_bytes=64)
+            regroup(nc, grouped_of[b, g][:], planes_of[b, g][:])
+
+        def quantise_features(b, g):
+            if g == 0:
+                f_codes_of[b] = code_pool.tile([P, PASSES, BLOCK], U32, name="f_codes", align_bytes=64)
+                f_scales_of[b] = code_pool.tile([P, PASSES, BLOCK], U8, name="f_scales", align_bytes=64)
             nc.vector.quantize_mx(
-                out=f_codes[:, g, :].bitcast(FP8X4),
-                scales=f_scales[:, g, :],
-                in_=grouped[:].rearrange("p r t -> p (r t)"),
+                out=f_codes_of[b][:, g, :].bitcast(FP8X4),
+                scales=f_scales_of[b][:, g, :],
+                in_=grouped_of[b, g][:].rearrange("p r t -> p (r t)"),
             )
 
-        def product(acc, f_codes, f_scales, passes, first_col):
+        def product(acc, b, passes, first_col):
             cols = slice(first_col, first_col + P)
             for g in passes:
                 nc.tensor.matmul_mx(
                     out=acc[:],
                     lhsT=w_codes[:, g, cols].bitcast(FP8X4), lhsT_scale=w_scales[:, g, cols],
-                    rhs=f_codes[:, g, :].bitcast(FP8X4), rhs_scale=f_scales[:, g, :],
+                    rhs=f_codes_of[b][:, g, :].bitcast(FP8X4), rhs_scale=f_scales_of[b][:, g, :],
                     start=(g == passes[0]), stop=(g == passes[-1]),
                 )
 
@@ -224,68 +258,114 @@ def tile_vectormerge_pa_t_kernel(
                         rhs=ident_f32[:], is_transpose=True, start=(i == 0), stop=(i == NS - 1),
                     )
 
-        def merge(b, f_codes, f_scales):
-            all_passes = tuple(range(PASSES))
-            logits = []
+        def gate_tile(name):
+            gate[name] = gate_pool.tile([P, BLOCK], F32, name=name)
+            return gate[name]
+
+        def logits(b):
             for i in range(NS):
-                logit = psum_mx.tile([P, BLOCK], F32, name="logit%d" % i, tag="mx%d" % i)
-                product(logit, f_codes, f_scales, all_passes, OUT + i * OUT)
-                logits.append(logit)
-            biased0 = gate_pool.tile([P, BLOCK], F32)
+                gate["logit%d" % i] = psum_mx.tile([P, BLOCK], F32, name="logit%d" % i, tag="mx%d" % i)
+                product(gate["logit%d" % i], b, tuple(range(PASSES)), OUT + i * OUT)
             nc.scalar.activation(
-                out=biased0[:], in_=logits[0][:], func=ACT.Identity, bias=gate_bias[:, 0:1], scale=1.0
+                out=gate_tile("biased0")[:], in_=gate["logit0"][:], func=ACT.Identity,
+                bias=gate_bias[:, 0:1], scale=1.0,
             )
-            top01 = gate_pool.tile([P, BLOCK], F32)
+
+        def take_off_maximum():
             nc.vector.scalar_tensor_tensor(
-                out=top01[:], in0=logits[1][:], scalar=gate_bias[:, 1:2], in1=biased0[:],
-                op0=ALU.add, op1=ALU.max,
+                out=gate_tile("top01")[:], in0=gate["logit1"][:], scalar=gate_bias[:, 1:2],
+                in1=gate["biased0"][:], op0=ALU.add, op1=ALU.max,
             )
-            top = gate_pool.tile([P, BLOCK], F32)
             nc.vector.scalar_tensor_tensor(
-                out=top[:], in0=logits[2][:], scalar=gate_bias[:, 2:3], in1=top01[:],
-                op0=ALU.add, op1=ALU.max,
+                out=gate_tile("top")[:], in0=gate["logit2"][:], scalar=gate_bias[:, 2:3],
+                in1=gate["top01"][:], op0=ALU.add, op1=ALU.max,
             )
-            expo = []
-            for i in range(NS):
-                below = gate_pool.tile([P, BLOCK], F32, name="below%d" % i)
-                if i == 0:
-                    nc.vector.tensor_sub(out=below[:], in0=biased0[:], in1=top[:])
-                else:
-                    nc.vector.scalar_tensor_tensor(
-                        out=below[:], in0=logits[i][:], scalar=gate_bias[:, i : i + 1], in1=top[:],
-                        op0=ALU.add, op1=ALU.subtract,
-                    )
-                e = gate_pool.tile([P, BLOCK], F32, name="expo%d" % i)
-                nc.scalar.activation(out=e[:], in_=below[:], func=ACT.Exp)
-                expo.append(e)
-            weighted = []
-            for s in range(NS):
-                y = psum_mx.tile([P, BLOCK], F32, name="y%d" % s, tag="mx%d" % s)
-                product(y, f_codes, f_scales, PASSES_OF_STREAM[s], 0)
-                w = gate_pool.tile([P, BLOCK], F32, name="weighted%d" % s)
+            nc.vector.tensor_sub(out=gate_tile("below0")[:], in0=gate["biased0"][:], in1=gate["top"][:])
+            for i in range(1, NS):
                 nc.vector.scalar_tensor_tensor(
-                    out=w[:], in0=y[:], scalar=param[:, OUT_BIAS_ROW + s : OUT_BIAS_ROW + s + 1],
-                    in1=expo[s][:], op0=ALU.add, op1=ALU.mult,
+                    out=gate_tile("below%d" % i)[:], in0=gate["logit%d" % i][:],
+                    scalar=gate_bias[:, i : i + 1], in1=gate["top"][:], op0=ALU.add, op1=ALU.subtract,
                 )
-                weighted.append(w)
-            denom = psum_sn.tile([P, BLOCK], F32)
-            sum_transposed(denom, expo)
-            numer = psum_sn.tile([P, BLOCK], F32)
-            sum_transposed(numer, weighted)
-            inverse = gate_pool.tile([P, BLOCK], F32)
-            nc.vector.reciprocal(out=inverse[:], in_=denom[:])
-            merged = gate_pool.tile([P, BLOCK], F32)
-            nc.vector.tensor_mul(out=merged[:], in0=numer[:], in1=inverse[:])
+
+        def exponentials(b):
+            for i in range(NS):
+                nc.scalar.activation(
+                    out=gate_tile("expo%d" % i)[:], in_=gate["below%d" % i][:], func=ACT.Exp
+                )
+            for s in range(NS):
+                gate["y%d" % s] = psum_mx.tile([P, BLOCK], F32, name="y%d" % s, tag="mx%d" % s)
+                product(gate["y%d" % s], b, PASSES_OF_STREAM[s], 0)
+
+        def weigh():
+            for s in range(NS):
+                nc.vector.scalar_tensor_tensor(
+                    out=gate_tile("weighted%d" % s)[:], in0=gate["y%d" % s][:],
+                    scalar=param[:, OUT_BIAS_ROW + s : OUT_BIAS_ROW + s + 1],
+                    in1=gate["expo%d" % s][:], op0=ALU.add, op1=ALU.mult,
+                )
+
+        def sums():
+            gate["denom"] = psum_sn.tile([P, BLOCK], F32, name="denom")
+            sum_transposed(gate["denom"], [gate["expo%d" % i] for i in range(NS)])
+            gate["numer"] = psum_sn.tile([P, BLOCK], F32, name="numer")
+            sum_transposed(gate["numer"], [gate["weighted%d" % s] for s in range(NS)])
+            nc.scalar.activation(out=gate_tile("log_denom")[:], in_=gate["denom"][:], func=ACT.Ln)
+
+        def invert():
+            nc.scalar.activation(
+                out=gate_tile("inverse")[:], in_=gate["log_denom"][:], func=ACT.Exp, scale=-1.0
+            )
+
+        def finish(b):
+            merged = out_pool.tile([P, BLOCK], F32)
+            nc.vector.tensor_mul(out=merged[:], in0=gate["numer"][:], in1=gate["inverse"][:])
             nc.sync.dma_start(
                 out=out[b * BLOCK : (b + 1) * BLOCK, :].rearrange("(p t) n -> p (t n)", t=ROW_TILES),
                 in_=merged[:],
             )
 
-        for b in range(N_BLOCKS):
-            x_blk = load(b)
-            rstd, shift = statistics(x_blk)
-            f_codes = code_pool.tile([P, PASSES, BLOCK], U32, align_bytes=64)
-            f_scales = code_pool.tile([P, PASSES, BLOCK], U8, align_bytes=64)
-            for g in range(PASSES):
-                features(x_blk, rstd, shift, f_codes, f_scales, g)
-            merge(b, f_codes, f_scales)
+        def step(n):
+            def at(lag):
+                if 0 <= n - lag < N_BLOCKS * STEPS_PER_BLOCK:
+                    return divmod(n - lag, STEPS_PER_BLOCK)
+                return None
+
+            merging = at(MERGE_LAG)
+            if merging and merging[1] == 1:
+                take_off_maximum()
+            if merging and merging[1] == 2:
+                weigh()
+            if merging and merging[1] == 3:
+                invert()
+            if at(TRANSPOSE_LAG):
+                transpose_and_scale(*at(TRANSPOSE_LAG))
+            if at(QUANT_LAG):
+                quantise_features(*at(QUANT_LAG))
+            if at(REGROUP_LAG):
+                regroup_features(*at(REGROUP_LAG))
+            if at(NORM_LAG):
+                normalise(*at(NORM_LAG))
+            if at(0):
+                b, g = at(0)
+                statistics(b, g)
+                if g == PASSES - 1:
+                    row_scalars(b)
+                if g == 0 and b + 1 < N_BLOCKS:
+                    load(b + 1)
+            if merging and merging[1] == 0:
+                logits(merging[0])
+            if merging and merging[1] == 1:
+                exponentials(merging[0])
+            if merging and merging[1] == 2:
+                sums()
+            if merging and merging[1] == 3:
+                finish(merging[0])
+
+        load(0)
+        load_small_vectors()
+        load_weights()
+        for n in range(REGROUP_LAG):
+            step(n)
+        quantise_weights()
+        for n in range(REGROUP_LAG, N_STEPS):
+            step(n)

@@ -25,7 +25,9 @@ PASSES = K_ALL // K_PASS
 STREAM_OF_PASS = (0, 1, 2, 2)
 PASSES_OF_STREAM = ((0,), (1,), (2, 3))
 W_COLS = OUT + NS * OUT
+LAST_GATE_COL = W_COLS - OUT
 EPS = 1e-5
+VECTOR_ROW_TILES = 1
 
 LN_W_ROW = 0
 LN_B_ROW = K_ALL // P
@@ -36,7 +38,7 @@ PARAM_ROWS = GATE_BIAS_ROW + NS * NS
 FLOPS = 2 * ROWS * K_ALL * W_COLS
 
 STEPS_PER_BLOCK = PASSES
-NORM_LAG = 5
+NORM_LAG = 3
 TRANSPOSE_LAG = NORM_LAG + 1
 REGROUP_LAG = TRANSPOSE_LAG + 1
 QUANT_LAG = REGROUP_LAG + 1
@@ -69,9 +71,10 @@ def tile_vectormerge_pa_t_kernel(
 
     with ExitStack() as ctx:
         keep = ctx.enter_context(tc.tile_pool(name="keep", bufs=1))
-        x_pool = ctx.enter_context(tc.tile_pool(name="x_pool", bufs=4))
-        stat_pool = ctx.enter_context(tc.tile_pool(name="stat_pool", bufs=3))
-        norm_pool = ctx.enter_context(tc.tile_pool(name="norm_pool", bufs=3))
+        x_pool = ctx.enter_context(tc.tile_pool(name="x_pool", bufs=3))
+        stat_pool = ctx.enter_context(tc.tile_pool(name="stat_pool", bufs=6))
+        norm_pool = ctx.enter_context(tc.tile_pool(name="norm_pool", bufs=4))
+        plane_pool = ctx.enter_context(tc.tile_pool(name="plane_pool", bufs=3))
         f_pool = ctx.enter_context(tc.tile_pool(name="f_pool", bufs=2))
         code_pool = ctx.enter_context(tc.tile_pool(name="code_pool", bufs=2))
         gate_pool = ctx.enter_context(tc.tile_pool(name="gate_pool", bufs=1))
@@ -86,12 +89,13 @@ def tile_vectormerge_pa_t_kernel(
         make_identity(nc, ident_f32[:])
         ident_bf16 = keep.tile([P, P], BF16)
         make_identity(nc, ident_bf16[:])
-        minus_half = keep.tile([P, ROW_TILES, NS], F32)
+        minus_half = keep.tile([P, ROW_TILES], F32)
         nc.vector.memset(minus_half[:], -0.5)
         param_rows = keep.tile([P, P], BF16)
         nc.vector.memset(param_rows[:], 0.0)
         param = keep.tile([P, P], F32)
         gate_bias = keep.tile([P, NS], F32)
+        diff_bias = keep.tile([P, NS - 1], F32)
         w_raw = keep.tile([P, PASSES, PACK, W_COLS], BF16)
         w_grouped = keep.tile([P, PASSES, W_COLS, PACK], BF16, align_bytes=64)
         w_codes = keep.tile([P, PASSES, W_COLS], U32, align_bytes=64)
@@ -130,6 +134,11 @@ def tile_vectormerge_pa_t_kernel(
                 in0=gate_bias[:],
                 in1=param[:, GATE_BIAS_ROW + 2 * NS : GATE_BIAS_ROW + 3 * NS],
             )
+            for i in range(NS - 1):
+                nc.gpsimd.tensor_sub(
+                    out=diff_bias[:, i : i + 1], in0=gate_bias[:, i : i + 1],
+                    in1=gate_bias[:, NS - 1 : NS],
+                )
 
         def load_weights():
             for s in range(NS):
@@ -144,6 +153,10 @@ def tile_vectormerge_pa_t_kernel(
                 )
 
         def quantise_weights():
+            nc.vector.tensor_scalar_mul(
+                out=w_raw[:, :, :, LAST_GATE_COL:W_COLS], in0=w_raw[:, :, :, LAST_GATE_COL:W_COLS],
+                scalar1=-1.0,
+            )
             for g in range(PASSES):
                 regroup(nc, w_grouped[:, g, :, :], w_raw[:, g, :, :])
             for g in range(PASSES):
@@ -155,8 +168,8 @@ def tile_vectormerge_pa_t_kernel(
 
         x_blks = {}
         partials = {}
-        neg_means = {}
         rstds = {}
+        shifts = {}
         x_norms = {}
         planes_of = {}
         grouped_of = {}
@@ -183,35 +196,44 @@ def tile_vectormerge_pa_t_kernel(
                     out=partials[b][:, t, g, :], in_=x_blks[b][:, t, g * K_PASS : (g + 1) * K_PASS]
                 )
 
-        def row_scalars(b):
-            mean_var = stat_pool.tile([P, ROW_TILES, NS, 2], F32)
+        def row_scalars(b, s):
+            g0 = PASSES_OF_STREAM[s][0]
+            g1 = PASSES_OF_STREAM[s][-1] + 1
+            mean_var = stat_pool.tile([P, ROW_TILES, 2], F32)
             for t in range(ROW_TILES):
-                for s in range(NS):
-                    g0 = PASSES_OF_STREAM[s][0]
-                    g1 = PASSES_OF_STREAM[s][-1] + 1
-                    nc.vector.bn_aggr(
-                        out=mean_var[:, t, s, :],
-                        in_=partials[b][:, t, g0:g1, :].rearrange("p g v -> p (g v)"),
-                    )
-            var_eps = stat_pool.tile([P, ROW_TILES, NS], F32)
-            nc.vector.tensor_scalar_add(out=var_eps[:], in0=mean_var[:, :, :, 1], scalar1=EPS)
-            neg_means[b] = stat_pool.tile([P, ROW_TILES, NS], F32, name="neg_mean")
-            nc.vector.tensor_scalar_mul(out=neg_means[b][:], in0=mean_var[:, :, :, 0], scalar1=-1.0)
-            rstds[b] = stat_pool.tile([P, ROW_TILES, NS], F32, name="rstd")
-            nc.gpsimd.tensor_tensor(out=rstds[b][:], in0=var_eps[:], in1=minus_half[:], op=ALU.pow)
+                nc.vector.bn_aggr(
+                    out=mean_var[:, t, :],
+                    in_=partials[b][:, t, g0:g1, :].rearrange("p g v -> p (g v)"),
+                )
+            var_eps = stat_pool.tile([P, ROW_TILES], F32)
+            nc.vector.tensor_scalar_add(out=var_eps[:], in0=mean_var[:, :, 1], scalar1=EPS)
+            neg_mean = stat_pool.tile([P, ROW_TILES], F32)
+            nc.vector.tensor_scalar_mul(out=neg_mean[:], in0=mean_var[:, :, 0], scalar1=-1.0)
+            rstds[b, s] = stat_pool.tile([P, ROW_TILES], F32, name="rstd")
+            nc.gpsimd.tensor_tensor(out=rstds[b, s][:], in0=var_eps[:], in1=minus_half[:], op=ALU.pow)
+            shifts[b, s] = stat_pool.tile([P, ROW_TILES], F32, name="shift")
+            nc.gpsimd.tensor_mul(out=shifts[b, s][:], in0=neg_mean[:], in1=rstds[b, s][:])
 
         def normalise(b, g):
             s = STREAM_OF_PASS[g]
             x_norms[b, g] = norm_pool.tile([P, ROW_TILES, K_PASS], F32, name="x_norm")
             for t in range(ROW_TILES):
-                nc.gpsimd.tensor_scalar(
-                    out=x_norms[b, g][:, t, :], in0=x_blks[b][:, t, g * K_PASS : (g + 1) * K_PASS],
-                    scalar1=neg_means[b][:, t, s : s + 1], scalar2=rstds[b][:, t, s : s + 1],
-                    op0=ALU.add, op1=ALU.mult,
-                )
+                x_rows = x_blks[b][:, t, g * K_PASS : (g + 1) * K_PASS]
+                rstd = rstds[b, s][:, t : t + 1]
+                shift = shifts[b, s][:, t : t + 1]
+                if t < VECTOR_ROW_TILES:
+                    nc.vector.tensor_scalar(
+                        out=x_norms[b, g][:, t, :], in0=x_rows, scalar1=rstd, scalar2=shift,
+                        op0=ALU.mult, op1=ALU.add,
+                    )
+                else:
+                    nc.scalar.activation(
+                        out=x_norms[b, g][:, t, :], in_=x_rows, func=ACT.Identity,
+                        scale=rstd, bias=shift,
+                    )
 
         def transpose_and_scale(b, g):
-            planes_of[b, g] = f_pool.tile([P, PACK, BLOCK], BF16, name="planes")
+            planes_of[b, g] = plane_pool.tile([P, PACK, BLOCK], BF16, name="planes")
             for j in range(PACK):
                 chunk = g * PACK + j
                 x_t = psum_xt.tile([P, BLOCK], F32, tag="xt")
@@ -240,14 +262,14 @@ def tile_vectormerge_pa_t_kernel(
                 in_=grouped_of[b, g][:].rearrange("p r t -> p (r t)"),
             )
 
-        def product(acc, b, passes, first_col):
-            cols = slice(first_col, first_col + P)
-            for g in passes:
+        def product(acc, b, passes, first_cols):
+            terms = [(g, c) for g in passes for c in first_cols]
+            for g, c in terms:
                 nc.tensor.matmul_mx(
                     out=acc[:],
-                    lhsT=w_codes[:, g, cols].bitcast(FP8X4), lhsT_scale=w_scales[:, g, cols],
+                    lhsT=w_codes[:, g, c : c + P].bitcast(FP8X4), lhsT_scale=w_scales[:, g, c : c + P],
                     rhs=f_codes_of[b][:, g, :].bitcast(FP8X4), rhs_scale=f_scales_of[b][:, g, :],
-                    start=(g == passes[0]), stop=(g == passes[-1]),
+                    start=((g, c) == terms[0]), stop=((g, c) == terms[-1]),
                 )
 
         def sum_transposed(acc, terms):
@@ -262,39 +284,38 @@ def tile_vectormerge_pa_t_kernel(
             gate[name] = gate_pool.tile([P, BLOCK], F32, name=name)
             return gate[name]
 
-        def logits(b):
-            for i in range(NS):
-                gate["logit%d" % i] = psum_mx.tile([P, BLOCK], F32, name="logit%d" % i, tag="mx%d" % i)
-                product(gate["logit%d" % i], b, tuple(range(PASSES)), OUT + i * OUT)
+        def logit_difference(b, i):
+            gate["diff%d" % i] = psum_mx.tile([P, BLOCK], F32, name="diff%d" % i, tag="mx%d" % i)
+            product(gate["diff%d" % i], b, tuple(range(PASSES)), (OUT + i * OUT, LAST_GATE_COL))
+
+        def maximum_with_zero():
             nc.scalar.activation(
-                out=gate_tile("biased0")[:], in_=gate["logit0"][:], func=ACT.Identity,
-                bias=gate_bias[:, 0:1], scale=1.0,
+                out=gate_tile("top02")[:], in_=gate["diff0"][:], func=ACT.Relu,
+                bias=diff_bias[:, 0:1], scale=1.0,
             )
 
         def take_off_maximum():
             nc.vector.scalar_tensor_tensor(
-                out=gate_tile("top01")[:], in0=gate["logit1"][:], scalar=gate_bias[:, 1:2],
-                in1=gate["biased0"][:], op0=ALU.add, op1=ALU.max,
+                out=gate_tile("top")[:], in0=gate["diff1"][:], scalar=diff_bias[:, 1:2],
+                in1=gate["top02"][:], op0=ALU.add, op1=ALU.max,
             )
-            nc.vector.scalar_tensor_tensor(
-                out=gate_tile("top")[:], in0=gate["logit2"][:], scalar=gate_bias[:, 2:3],
-                in1=gate["top01"][:], op0=ALU.add, op1=ALU.max,
-            )
-            nc.vector.tensor_sub(out=gate_tile("below0")[:], in0=gate["biased0"][:], in1=gate["top"][:])
-            for i in range(1, NS):
+            for i in range(NS - 1):
                 nc.vector.scalar_tensor_tensor(
-                    out=gate_tile("below%d" % i)[:], in0=gate["logit%d" % i][:],
-                    scalar=gate_bias[:, i : i + 1], in1=gate["top"][:], op0=ALU.add, op1=ALU.subtract,
+                    out=gate_tile("below%d" % i)[:], in0=gate["diff%d" % i][:],
+                    scalar=diff_bias[:, i : i + 1], in1=gate["top"][:], op0=ALU.add, op1=ALU.subtract,
                 )
 
         def exponentials(b):
-            for i in range(NS):
+            for i in range(NS - 1):
                 nc.scalar.activation(
                     out=gate_tile("expo%d" % i)[:], in_=gate["below%d" % i][:], func=ACT.Exp
                 )
+            nc.scalar.activation(
+                out=gate_tile("expo%d" % (NS - 1))[:], in_=gate["top"][:], func=ACT.Exp, scale=-1.0
+            )
             for s in range(NS):
                 gate["y%d" % s] = psum_mx.tile([P, BLOCK], F32, name="y%d" % s, tag="mx%d" % s)
-                product(gate["y%d" % s], b, PASSES_OF_STREAM[s], 0)
+                product(gate["y%d" % s], b, PASSES_OF_STREAM[s], (0,))
 
         def weigh():
             for s in range(NS):
@@ -304,9 +325,11 @@ def tile_vectormerge_pa_t_kernel(
                     in1=gate["expo%d" % s][:], op0=ALU.add, op1=ALU.mult,
                 )
 
-        def sums():
+        def denominator():
             gate["denom"] = psum_sn.tile([P, BLOCK], F32, name="denom")
             sum_transposed(gate["denom"], [gate["expo%d" % i] for i in range(NS)])
+
+        def numerator():
             gate["numer"] = psum_sn.tile([P, BLOCK], F32, name="numer")
             sum_transposed(gate["numer"], [gate["weighted%d" % s] for s in range(NS)])
             nc.scalar.activation(out=gate_tile("log_denom")[:], in_=gate["denom"][:], func=ACT.Ln)
@@ -331,33 +354,37 @@ def tile_vectormerge_pa_t_kernel(
                 return None
 
             merging = at(MERGE_LAG)
+            if merging and merging[1] == 0:
+                logit_difference(merging[0], 0)
             if merging and merging[1] == 1:
                 take_off_maximum()
             if merging and merging[1] == 2:
                 weigh()
+                denominator()
             if merging and merging[1] == 3:
                 invert()
+            if at(NORM_LAG):
+                normalise(*at(NORM_LAG))
             if at(TRANSPOSE_LAG):
                 transpose_and_scale(*at(TRANSPOSE_LAG))
             if at(QUANT_LAG):
                 quantise_features(*at(QUANT_LAG))
-            if at(REGROUP_LAG):
-                regroup_features(*at(REGROUP_LAG))
-            if at(NORM_LAG):
-                normalise(*at(NORM_LAG))
             if at(0):
                 b, g = at(0)
                 statistics(b, g)
-                if g == PASSES - 1:
-                    row_scalars(b)
+                if g == PASSES_OF_STREAM[STREAM_OF_PASS[g]][-1]:
+                    row_scalars(b, STREAM_OF_PASS[g])
                 if g == 0 and b + 1 < N_BLOCKS:
                     load(b + 1)
+            if at(REGROUP_LAG):
+                regroup_features(*at(REGROUP_LAG))
             if merging and merging[1] == 0:
-                logits(merging[0])
+                logit_difference(merging[0], 1)
+                maximum_with_zero()
             if merging and merging[1] == 1:
                 exponentials(merging[0])
             if merging and merging[1] == 2:
-                sums()
+                numerator()
             if merging and merging[1] == 3:
                 finish(merging[0])
 

@@ -38,7 +38,8 @@ PARAM_ROWS = GATE_BIAS_ROW + NS * NS
 FLOPS = 2 * ROWS * K_ALL * W_COLS
 
 STEPS_PER_BLOCK = PASSES
-NORM_LAG = 3
+AGGREGATE_LAG = 1
+NORM_LAG = 4
 TRANSPOSE_LAG = NORM_LAG + 1
 REGROUP_LAG = TRANSPOSE_LAG + 1
 QUANT_LAG = REGROUP_LAG + 1
@@ -206,9 +207,9 @@ def tile_vectormerge_pa_t_kernel(
                     in_=partials[b][:, t, g0:g1, :].rearrange("p g v -> p (g v)"),
                 )
             var_eps = stat_pool.tile([P, ROW_TILES], F32)
-            nc.vector.tensor_scalar_add(out=var_eps[:], in0=mean_var[:, :, 1], scalar1=EPS)
+            nc.gpsimd.tensor_scalar_add(out=var_eps[:], in0=mean_var[:, :, 1], scalar1=EPS)
             neg_mean = stat_pool.tile([P, ROW_TILES], F32)
-            nc.vector.tensor_scalar_mul(out=neg_mean[:], in0=mean_var[:, :, 0], scalar1=-1.0)
+            nc.gpsimd.tensor_scalar_mul(out=neg_mean[:], in0=mean_var[:, :, 0], scalar1=-1.0)
             rstds[b, s] = stat_pool.tile([P, ROW_TILES], F32, name="rstd")
             nc.gpsimd.tensor_tensor(out=rstds[b, s][:], in0=var_eps[:], in1=minus_half[:], op=ALU.pow)
             shifts[b, s] = stat_pool.tile([P, ROW_TILES], F32, name="shift")
@@ -294,11 +295,13 @@ def tile_vectormerge_pa_t_kernel(
                 bias=diff_bias[:, 0:1], scale=1.0,
             )
 
-        def take_off_maximum():
+        def maximum():
             nc.vector.scalar_tensor_tensor(
                 out=gate_tile("top")[:], in0=gate["diff1"][:], scalar=diff_bias[:, 1:2],
                 in1=gate["top02"][:], op0=ALU.add, op1=ALU.max,
             )
+
+        def take_off_maximum():
             for i in range(NS - 1):
                 nc.vector.scalar_tensor_tensor(
                     out=gate_tile("below%d" % i)[:], in0=gate["diff%d" % i][:],
@@ -357,7 +360,7 @@ def tile_vectormerge_pa_t_kernel(
             if merging and merging[1] == 0:
                 logit_difference(merging[0], 0)
             if merging and merging[1] == 1:
-                take_off_maximum()
+                maximum()
             if merging and merging[1] == 2:
                 weigh()
                 denominator()
@@ -369,11 +372,15 @@ def tile_vectormerge_pa_t_kernel(
                 transpose_and_scale(*at(TRANSPOSE_LAG))
             if at(QUANT_LAG):
                 quantise_features(*at(QUANT_LAG))
+            if merging and merging[1] == 1:
+                take_off_maximum()
+            if at(AGGREGATE_LAG):
+                b, g = at(AGGREGATE_LAG)
+                if g == PASSES_OF_STREAM[STREAM_OF_PASS[g]][-1]:
+                    row_scalars(b, STREAM_OF_PASS[g])
             if at(0):
                 b, g = at(0)
                 statistics(b, g)
-                if g == PASSES_OF_STREAM[STREAM_OF_PASS[g]][-1]:
-                    row_scalars(b, STREAM_OF_PASS[g])
                 if g == 0 and b + 1 < N_BLOCKS:
                     load(b + 1)
             if at(REGROUP_LAG):

@@ -38,12 +38,14 @@ PARAM_ROWS = GATE_BIAS_ROW + NS * NS
 FLOPS = 2 * ROWS * K_ALL * W_COLS
 
 STEPS_PER_BLOCK = PASSES
-AGGREGATE_LAG = 1
-NORM_LAG = 4
+LOG_LAG = STEPS_PER_BLOCK
+RSTD_LAG = LOG_LAG + 1
+NORM_LAG = RSTD_LAG + 1
 TRANSPOSE_LAG = NORM_LAG + 1
 REGROUP_LAG = TRANSPOSE_LAG + 1
 QUANT_LAG = REGROUP_LAG + 1
-MERGE_LAG = QUANT_LAG + STEPS_PER_BLOCK
+MERGE_LAG = QUANT_LAG + STEPS_PER_BLOCK + 1
+assert (MERGE_LAG + 2 - LOG_LAG) % STEPS_PER_BLOCK == 0
 N_STEPS = N_BLOCKS * STEPS_PER_BLOCK + MERGE_LAG
 
 
@@ -72,15 +74,15 @@ def tile_vectormerge_pa_t_kernel(
 
     with ExitStack() as ctx:
         keep = ctx.enter_context(tc.tile_pool(name="keep", bufs=1))
-        x_pool = ctx.enter_context(tc.tile_pool(name="x_pool", bufs=3))
-        stat_pool = ctx.enter_context(tc.tile_pool(name="stat_pool", bufs=6))
+        x_pool = ctx.enter_context(tc.tile_pool(name="x_pool", bufs=4))
+        stat_pool = ctx.enter_context(tc.tile_pool(name="stat_pool", bufs=3))
         norm_pool = ctx.enter_context(tc.tile_pool(name="norm_pool", bufs=4))
         plane_pool = ctx.enter_context(tc.tile_pool(name="plane_pool", bufs=3))
         f_pool = ctx.enter_context(tc.tile_pool(name="f_pool", bufs=2))
         code_pool = ctx.enter_context(tc.tile_pool(name="code_pool", bufs=2))
         gate_pool = ctx.enter_context(tc.tile_pool(name="gate_pool", bufs=1))
         out_pool = ctx.enter_context(tc.tile_pool(name="out_pool", bufs=2))
-        psum_xt = ctx.enter_context(tc.psum_pool(name="psum_xt", bufs=3))
+        psum_xt = ctx.enter_context(tc.psum_pool(name="psum_xt", bufs=4))
         psum_mx = ctx.enter_context(tc.psum_pool(name="psum_mx", bufs=1))
         psum_sn = ctx.enter_context(tc.psum_pool(name="psum_sn", bufs=1))
 
@@ -90,8 +92,6 @@ def tile_vectormerge_pa_t_kernel(
         make_identity(nc, ident_f32[:])
         ident_bf16 = keep.tile([P, P], BF16)
         make_identity(nc, ident_bf16[:])
-        minus_half = keep.tile([P, ROW_TILES], F32)
-        nc.vector.memset(minus_half[:], -0.5)
         param_rows = keep.tile([P, P], BF16)
         nc.vector.memset(param_rows[:], 0.0)
         param = keep.tile([P, P], F32)
@@ -169,6 +169,9 @@ def tile_vectormerge_pa_t_kernel(
 
         x_blks = {}
         partials = {}
+        mean_vars = {}
+        var_epss = {}
+        log_vars = {}
         rstds = {}
         shifts = {}
         x_norms = {}
@@ -190,38 +193,51 @@ def tile_vectormerge_pa_t_kernel(
                 )
 
         def statistics(b, g):
+            s = STREAM_OF_PASS[g]
             if g == 0:
                 partials[b] = stat_pool.tile([P, ROW_TILES, PASSES, 6], F32, name="partial")
+                mean_vars[b] = stat_pool.tile([P, NS, ROW_TILES, 2], F32, name="mean_var")
             for t in range(ROW_TILES):
                 nc.vector.bn_stats(
                     out=partials[b][:, t, g, :], in_=x_blks[b][:, t, g * K_PASS : (g + 1) * K_PASS]
                 )
-
-        def row_scalars(b, s):
-            g0 = PASSES_OF_STREAM[s][0]
-            g1 = PASSES_OF_STREAM[s][-1] + 1
-            mean_var = stat_pool.tile([P, ROW_TILES, 2], F32)
-            for t in range(ROW_TILES):
-                nc.vector.bn_aggr(
-                    out=mean_var[:, t, :],
-                    in_=partials[b][:, t, g0:g1, :].rearrange("p g v -> p (g v)"),
+            if g == PASSES_OF_STREAM[s][-1]:
+                g0 = PASSES_OF_STREAM[s][0]
+                for t in range(ROW_TILES):
+                    nc.vector.bn_aggr(
+                        out=mean_vars[b][:, s, t, :],
+                        in_=partials[b][:, t, g0 : g + 1, :].rearrange("p g v -> p (g v)"),
+                    )
+            if g == PASSES - 1:
+                var_epss[b] = stat_pool.tile([P, NS, ROW_TILES], F32, name="var_eps")
+                nc.vector.tensor_scalar_add(
+                    out=var_epss[b][:], in0=mean_vars[b][:, :, :, 1], scalar1=EPS
                 )
-            var_eps = stat_pool.tile([P, ROW_TILES], F32)
-            nc.gpsimd.tensor_scalar_add(out=var_eps[:], in0=mean_var[:, :, 1], scalar1=EPS)
-            neg_mean = stat_pool.tile([P, ROW_TILES], F32)
-            nc.gpsimd.tensor_scalar_mul(out=neg_mean[:], in0=mean_var[:, :, 0], scalar1=-1.0)
-            rstds[b, s] = stat_pool.tile([P, ROW_TILES], F32, name="rstd")
-            nc.gpsimd.tensor_tensor(out=rstds[b, s][:], in0=var_eps[:], in1=minus_half[:], op=ALU.pow)
-            shifts[b, s] = stat_pool.tile([P, ROW_TILES], F32, name="shift")
-            nc.gpsimd.tensor_mul(out=shifts[b, s][:], in0=neg_mean[:], in1=rstds[b, s][:])
+
+        def log_variance(b):
+            log_vars[b] = stat_pool.tile([P, NS, ROW_TILES], F32, name="log_var")
+            nc.scalar.activation(
+                out=log_vars[b][:], in_=var_epss[b][:], func=ACT.Ln
+            )
+
+        def rstd_of(b):
+            rstds[b] = stat_pool.tile([P, NS, ROW_TILES], F32, name="rstd")
+            nc.scalar.activation(out=rstds[b][:], in_=log_vars[b][:], func=ACT.Exp, scale=-0.5)
+
+        def shift_of(b):
+            shifts[b] = stat_pool.tile([P, NS, ROW_TILES], F32, name="shift")
+            nc.vector.scalar_tensor_tensor(
+                out=shifts[b][:], in0=mean_vars[b][:, :, :, 0], scalar=-1.0, in1=rstds[b][:],
+                op0=ALU.mult, op1=ALU.mult,
+            )
 
         def normalise(b, g):
             s = STREAM_OF_PASS[g]
             x_norms[b, g] = norm_pool.tile([P, ROW_TILES, K_PASS], F32, name="x_norm")
             for t in range(ROW_TILES):
                 x_rows = x_blks[b][:, t, g * K_PASS : (g + 1) * K_PASS]
-                rstd = rstds[b, s][:, t : t + 1]
-                shift = shifts[b, s][:, t : t + 1]
+                rstd = rstds[b][:, s, t : t + 1]
+                shift = shifts[b][:, s, t : t + 1]
                 if t < VECTOR_ROW_TILES:
                     nc.vector.tensor_scalar(
                         out=x_norms[b, g][:, t, :], in0=x_rows, scalar1=rstd, scalar2=shift,
@@ -295,13 +311,11 @@ def tile_vectormerge_pa_t_kernel(
                 bias=diff_bias[:, 0:1], scale=1.0,
             )
 
-        def maximum():
+        def take_off_maximum():
             nc.vector.scalar_tensor_tensor(
                 out=gate_tile("top")[:], in0=gate["diff1"][:], scalar=diff_bias[:, 1:2],
                 in1=gate["top02"][:], op0=ALU.add, op1=ALU.max,
             )
-
-        def take_off_maximum():
             for i in range(NS - 1):
                 nc.vector.scalar_tensor_tensor(
                     out=gate_tile("below%d" % i)[:], in0=gate["diff%d" % i][:],
@@ -317,7 +331,10 @@ def tile_vectormerge_pa_t_kernel(
                 out=gate_tile("expo%d" % (NS - 1))[:], in_=gate["top"][:], func=ACT.Exp, scale=-1.0
             )
             for s in range(NS):
-                gate["y%d" % s] = psum_mx.tile([P, BLOCK], F32, name="y%d" % s, tag="mx%d" % s)
+                if s < NS - 1:
+                    gate["y%d" % s] = psum_mx.tile([P, BLOCK], F32, name="y%d" % s, tag="mx%d" % s)
+                else:
+                    gate["y%d" % s] = psum_sn.tile([P, BLOCK], F32, name="y%d" % s, tag="numer")
                 product(gate["y%d" % s], b, PASSES_OF_STREAM[s], (0,))
 
         def weigh():
@@ -333,7 +350,7 @@ def tile_vectormerge_pa_t_kernel(
             sum_transposed(gate["denom"], [gate["expo%d" % i] for i in range(NS)])
 
         def numerator():
-            gate["numer"] = psum_sn.tile([P, BLOCK], F32, name="numer")
+            gate["numer"] = psum_sn.tile([P, BLOCK], F32, name="numer", tag="numer")
             sum_transposed(gate["numer"], [gate["weighted%d" % s] for s in range(NS)])
             nc.scalar.activation(out=gate_tile("log_denom")[:], in_=gate["denom"][:], func=ACT.Ln)
 
@@ -360,24 +377,20 @@ def tile_vectormerge_pa_t_kernel(
             if merging and merging[1] == 0:
                 logit_difference(merging[0], 0)
             if merging and merging[1] == 1:
-                maximum()
+                take_off_maximum()
             if merging and merging[1] == 2:
                 weigh()
                 denominator()
             if merging and merging[1] == 3:
                 invert()
+            if at(RSTD_LAG) and at(RSTD_LAG)[1] == 0:
+                rstd_of(at(RSTD_LAG)[0])
             if at(NORM_LAG):
                 normalise(*at(NORM_LAG))
             if at(TRANSPOSE_LAG):
                 transpose_and_scale(*at(TRANSPOSE_LAG))
             if at(QUANT_LAG):
                 quantise_features(*at(QUANT_LAG))
-            if merging and merging[1] == 1:
-                take_off_maximum()
-            if at(AGGREGATE_LAG):
-                b, g = at(AGGREGATE_LAG)
-                if g == PASSES_OF_STREAM[STREAM_OF_PASS[g]][-1]:
-                    row_scalars(b, STREAM_OF_PASS[g])
             if at(0):
                 b, g = at(0)
                 statistics(b, g)
@@ -392,6 +405,10 @@ def tile_vectormerge_pa_t_kernel(
                 exponentials(merging[0])
             if merging and merging[1] == 2:
                 numerator()
+            if at(LOG_LAG) and at(LOG_LAG)[1] == 0:
+                log_variance(at(LOG_LAG)[0])
+            if at(RSTD_LAG) and at(RSTD_LAG)[1] == 0:
+                shift_of(at(RSTD_LAG)[0])
             if merging and merging[1] == 3:
                 finish(merging[0])
 

from contextlib import ExitStack

import concourse.mybir as mybir
from concourse.masks import make_identity

F32 = mybir.dt.float32
BF16 = mybir.dt.bfloat16
U32 = mybir.dt.uint32
U8 = mybir.dt.uint8
FP8X4 = mybir.dt.float8_e4m3fn_x4
ALU = mybir.AluOpType
ACT = mybir.ActivationFunctionType

P = 128
PACK = 4
K_PASS = P * PACK
ROWS = 4096
BLOCK = 512
ROW_TILES = BLOCK // P
N_BLOCKS = ROWS // BLOCK
OUT = 128
NS = 3
K_ALL = 2048
PASSES = K_ALL // K_PASS
STREAM_OF_PASS = (0, 1, 2, 2)
PASSES_OF_STREAM = ((0,), (1,), (2, 3))
W_COLS = OUT + NS * OUT
LAST_GATE_COL = W_COLS - OUT
EPS = 1e-5
VECTOR_ROW_TILES = 1

LN_W_ROW = 0
LN_B_ROW = K_ALL // P
OUT_BIAS_ROW = 2 * (K_ALL // P)
GATE_BIAS_ROW = OUT_BIAS_ROW + NS
PARAM_ROWS = GATE_BIAS_ROW + NS * NS

FLOPS = 2 * ROWS * K_ALL * W_COLS

STEPS_PER_BLOCK = PASSES
LOG_LAG = STEPS_PER_BLOCK
RSTD_LAG = LOG_LAG + 1
NORM_LAG = RSTD_LAG + 1
TRANSPOSE_LAG = NORM_LAG + 1
REGROUP_LAG = TRANSPOSE_LAG + 1
QUANT_LAG = REGROUP_LAG + 1
MERGE_LAG = QUANT_LAG + STEPS_PER_BLOCK + 1
assert (MERGE_LAG + 2 - LOG_LAG) % STEPS_PER_BLOCK == 0
N_STEPS = N_BLOCKS * STEPS_PER_BLOCK + MERGE_LAG


def regroup(nc, grouped, planes):
    nc.vector.tensor_copy(
        out=grouped.rearrange("p (c i) t -> p c t i", i=4),
        in_=planes.rearrange("p t (c i) -> p c t i", i=4),
    )


def tile_vectormerge_pa_t_kernel(
    tc,
    x_a, ln_w_a, ln_b_a, W_a, b_a, Wg_a, bg_a,
    x_b, ln_w_b, ln_b_b, W_b, b_b, Wg_b, bg_b,
    x_c, ln_w_c, ln_b_c, W_c, b_c, Wg_c, bg_c,
    out,
):
    nc = tc.nc
    xs = (x_a, x_b, x_c)
    ln_ws = (ln_w_a, ln_w_b, ln_w_c)
    ln_bs = (ln_b_a, ln_b_b, ln_b_c)
    Ws = (W_a, W_b, W_c)
    bs = (b_a, b_b, b_c)
    Wgs = (Wg_a, Wg_b, Wg_c)
    bgs = (bg_a, bg_b, bg_c)

    with ExitStack() as ctx:
        keep = ctx.enter_context(tc.tile_pool(name="keep", bufs=1))
        x_pool = ctx.enter_context(tc.tile_pool(name="x_pool", bufs=4))
        stat_pool = ctx.enter_context(tc.tile_pool(name="stat_pool", bufs=3))
        norm_pool = ctx.enter_context(tc.tile_pool(name="norm_pool", bufs=4))
        plane_pool = ctx.enter_context(tc.tile_pool(name="plane_pool", bufs=3))
        f_pool = ctx.enter_context(tc.tile_pool(name="f_pool", bufs=2))
        code_pool = ctx.enter_context(tc.tile_pool(name="code_pool", bufs=2))
        gate_pool = ctx.enter_context(tc.tile_pool(name="gate_pool", bufs=1))
        out_pool = ctx.enter_context(tc.tile_pool(name="out_pool", bufs=2))
        psum_xt = ctx.enter_context(tc.psum_pool(name="psum_xt", bufs=4))
        psum_mx = ctx.enter_context(tc.psum_pool(name="psum_mx", bufs=1))
        psum_sn = ctx.enter_context(tc.psum_pool(name="psum_sn", bufs=1))

        ctx.enter_context(tc.manual_schedule())

        ident_f32 = keep.tile([P, P], F32)
        make_identity(nc, ident_f32[:])
        ident_bf16 = keep.tile([P, P], BF16)
        make_identity(nc, ident_bf16[:])
        param_rows = keep.tile([P, P], BF16)
        nc.vector.memset(param_rows[:], 0.0)
        param = keep.tile([P, P], F32)
        gate_bias = keep.tile([P, NS], F32)
        diff_bias = keep.tile([P, NS - 1], F32)
        w_raw = keep.tile([P, PASSES, PACK, W_COLS], BF16)
        w_grouped = keep.tile([P, PASSES, W_COLS, PACK], BF16, align_bytes=64)
        w_codes = keep.tile([P, PASSES, W_COLS], U32, align_bytes=64)
        w_scales = keep.tile([P, PASSES, W_COLS], U8, align_bytes=64)

        def load_small_vectors():
            for s in range(NS):
                first = PASSES_OF_STREAM[s][0] * PACK
                chunks = len(PASSES_OF_STREAM[s]) * PACK
                nc.sync.dma_start(
                    out=param_rows[LN_W_ROW + first : LN_W_ROW + first + chunks, :],
                    in_=ln_ws[s].rearrange("(c p) -> c p", p=P),
                )
                nc.sync.dma_start(
                    out=param_rows[LN_B_ROW + first : LN_B_ROW + first + chunks, :],
                    in_=ln_bs[s].rearrange("(c p) -> c p", p=P),
                )
                nc.sync.dma_start(
                    out=param_rows[OUT_BIAS_ROW + s : OUT_BIAS_ROW + s + 1, :],
                    in_=bs[s].rearrange("(c p) -> c p", p=P),
                )
                nc.sync.dma_start(
                    out=param_rows[GATE_BIAS_ROW + NS * s : GATE_BIAS_ROW + NS * (s + 1), :],
                    in_=bgs[s].rearrange("(c p) -> c p", p=P),
                )
            param_ps = psum_xt.tile([P, P], BF16, tag="xt")
            nc.tensor.transpose(param_ps[:], param_rows[:], ident_bf16[:])
            nc.scalar.copy(out=param[:], in_=param_ps[:])
            nc.gpsimd.tensor_add(
                out=gate_bias[:],
                in0=param[:, GATE_BIAS_ROW : GATE_BIAS_ROW + NS],
                in1=param[:, GATE_BIAS_ROW + NS : GATE_BIAS_ROW + 2 * NS],
            )
            nc.gpsimd.tensor_add(
                out=gate_bias[:],
                in0=gate_bias[:],
                in1=param[:, GATE_BIAS_ROW + 2 * NS : GATE_BIAS_ROW + 3 * NS],
            )
            for i in range(NS - 1):
                nc.gpsimd.tensor_sub(
                    out=diff_bias[:, i : i + 1], in0=gate_bias[:, i : i + 1],
                    in1=gate_bias[:, NS - 1 : NS],
                )

        def load_weights():
            for s in range(NS):
                g0 = PASSES_OF_STREAM[s][0]
                g1 = PASSES_OF_STREAM[s][-1] + 1
                rows_view = w_raw[:, g0:g1, :, :].rearrange("p g t n -> p (g t) n")
                nc.sync.dma_start(
                    out=rows_view[:, :, 0:OUT], in_=Ws[s].rearrange("(c p) n -> p c n", p=P)
                )
                nc.sync.dma_start(
                    out=rows_view[:, :, OUT:W_COLS], in_=Wgs[s].rearrange("(c p) n -> p c n", p=P)
                )

        def quantise_weights():
            nc.vector.tensor_scalar_mul(
                out=w_raw[:, :, :, LAST_GATE_COL:W_COLS], in0=w_raw[:, :, :, LAST_GATE_COL:W_COLS],
                scalar1=-1.0,
            )
            for g in range(PASSES):
                regroup(nc, w_grouped[:, g, :, :], w_raw[:, g, :, :])
            for g in range(PASSES):
                nc.vector.quantize_mx(
                    out=w_codes[:, g, :].bitcast(FP8X4),
                    scales=w_scales[:, g, :],
                    in_=w_grouped[:, g, :, :].rearrange("p n t -> p (n t)"),
                )

        x_blks = {}
        partials = {}
        mean_vars = {}
        var_epss = {}
        log_vars = {}
        rstds = {}
        shifts = {}
        x_norms = {}
        planes_of = {}
        grouped_of = {}
        f_codes_of = {}
        f_scales_of = {}
        gate = {}

        def load(b):
            x_blks[b] = x_pool.tile([P, ROW_TILES, K_ALL], BF16, name="x_blk")
            rows = slice(b * BLOCK, (b + 1) * BLOCK)
            for s in range(NS):
                k0 = PASSES_OF_STREAM[s][0] * K_PASS
                k1 = (PASSES_OF_STREAM[s][-1] + 1) * K_PASS
                nc.sync.dma_start(
                    out=x_blks[b][:, :, k0:k1],
                    in_=xs[s][rows, :].rearrange("(p t) k -> p t k", t=ROW_TILES),
                )

        def statistics(b, g):
            s = STREAM_OF_PASS[g]
            if g == 0:
                partials[b] = stat_pool.tile([P, ROW_TILES, PASSES, 6], F32, name="partial")
                mean_vars[b] = stat_pool.tile([P, NS, ROW_TILES, 2], F32, name="mean_var")
            for t in range(ROW_TILES):
                nc.vector.bn_stats(
                    out=partials[b][:, t, g, :], in_=x_blks[b][:, t, g * K_PASS : (g + 1) * K_PASS]
                )
            if g == PASSES_OF_STREAM[s][-1]:
                g0 = PASSES_OF_STREAM[s][0]
                for t in range(ROW_TILES):
                    nc.vector.bn_aggr(
                        out=mean_vars[b][:, s, t, :],
                        in_=partials[b][:, t, g0 : g + 1, :].rearrange("p g v -> p (g v)"),
                    )
            if g == PASSES - 1:
                var_epss[b] = stat_pool.tile([P, NS, ROW_TILES], F32, name="var_eps")
                nc.vector.tensor_scalar_add(
                    out=var_epss[b][:], in0=mean_vars[b][:, :, :, 1], scalar1=EPS
                )

        def log_variance(b):
            log_vars[b] = stat_pool.tile([P, NS, ROW_TILES], F32, name="log_var")
            nc.scalar.activation(
                out=log_vars[b][:], in_=var_epss[b][:], func=ACT.Ln
            )

        def rstd_of(b):
            rstds[b] = stat_pool.tile([P, NS, ROW_TILES], F32, name="rstd")
            nc.scalar.activation(out=rstds[b][:], in_=log_vars[b][:], func=ACT.Exp, scale=-0.5)

        def shift_of(b):
            shifts[b] = stat_pool.tile([P, NS, ROW_TILES], F32, name="shift")
            nc.vector.scalar_tensor_tensor(
                out=shifts[b][:], in0=mean_vars[b][:, :, :, 0], scalar=-1.0, in1=rstds[b][:],
                op0=ALU.mult, op1=ALU.mult,
            )

        def normalise(b, g):
            s = STREAM_OF_PASS[g]
            x_norms[b, g] = norm_pool.tile([P, ROW_TILES, K_PASS], F32, name="x_norm")
            for t in range(ROW_TILES):
                x_rows = x_blks[b][:, t, g * K_PASS : (g + 1) * K_PASS]
                rstd = rstds[b][:, s, t : t + 1]
                shift = shifts[b][:, s, t : t + 1]
                if t < VECTOR_ROW_TILES:
                    nc.vector.tensor_scalar(
                        out=x_norms[b, g][:, t, :], in0=x_rows, scalar1=rstd, scalar2=shift,
                        op0=ALU.mult, op1=ALU.add,
                    )
                else:
                    nc.scalar.activation(
                        out=x_norms[b, g][:, t, :], in_=x_rows, func=ACT.Identity,
                        scale=rstd, bias=shift,
                    )

        def transpose_and_scale(b, g):
            planes_of[b, g] = plane_pool.tile([P, PACK, BLOCK], BF16, name="planes")
            for j in range(PACK):
                chunk = g * PACK + j
                x_t = psum_xt.tile([P, BLOCK], F32, tag="xt")
                for t in range(ROW_TILES):
                    nc.tensor.transpose(
                        x_t[:, t * P : (t + 1) * P], x_norms[b, g][:, t, j * P : (j + 1) * P],
                        ident_f32[:],
                    )
                nc.scalar.activation(
                    out=planes_of[b, g][:, j, :], in_=x_t[:], func=ACT.Relu,
                    scale=param[:, LN_W_ROW + chunk : LN_W_ROW + chunk + 1],
                    bias=param[:, LN_B_ROW + chunk : LN_B_ROW + chunk + 1],
                )

        def regroup_features(b, g):
            grouped_of[b, g] = f_pool.tile([P, BLOCK, PACK], BF16, name="grouped", align_bytes=64)
            regroup(nc, grouped_of[b, g][:], planes_of[b, g][:])

        def quantise_features(b, g):
            if g == 0:
                f_codes_of[b] = code_pool.tile([P, PASSES, BLOCK], U32, name="f_codes", align_bytes=64)
                f_scales_of[b] = code_pool.tile([P, PASSES, BLOCK], U8, name="f_scales", align_bytes=64)
            nc.vector.quantize_mx(
                out=f_codes_of[b][:, g, :].bitcast(FP8X4),
                scales=f_scales_of[b][:, g, :],
                in_=grouped_of[b, g][:].rearrange("p r t -> p (r t)"),
            )

        def product(acc, b, passes, first_cols):
            terms = [(g, c) for g in passes for c in first_cols]
            for g, c in terms:
                nc.tensor.matmul_mx(
                    out=acc[:],
                    lhsT=w_codes[:, g, c : c + P].bitcast(FP8X4), lhsT_scale=w_scales[:, g, c : c + P],
                    rhs=f_codes_of[b][:, g, :].bitcast(FP8X4), rhs_scale=f_scales_of[b][:, g, :],
                    start=((g, c) == terms[0]), stop=((g, c) == terms[-1]),
                )

        def sum_transposed(acc, terms):
            for t in range(ROW_TILES):
                for i in range(NS):
                    nc.tensor.matmul(
                        out=acc[:, t * P : (t + 1) * P], lhsT=terms[i][:, t * P : (t + 1) * P],
                        rhs=ident_f32[:], is_transpose=True, start=(i == 0), stop=(i == NS - 1),
                    )

        def gate_tile(name):
            gate[name] = gate_pool.tile([P, BLOCK], F32, name=name)
            return gate[name]

        def logit_difference(b, i):
            gate["diff%d" % i] = psum_mx.tile([P, BLOCK], F32, name="diff%d" % i, tag="mx%d" % i)
            product(gate["diff%d" % i], b, tuple(range(PASSES)), (OUT + i * OUT, LAST_GATE_COL))

        def maximum_with_zero():
            nc.scalar.activation(
                out=gate_tile("top02")[:], in_=gate["diff0"][:], func=ACT.Relu,
                bias=diff_bias[:, 0:1], scale=1.0,
            )

        def take_off_maximum():
            nc.vector.scalar_tensor_tensor(
                out=gate_tile("top")[:], in0=gate["diff1"][:], scalar=diff_bias[:, 1:2],
                in1=gate["top02"][:], op0=ALU.add, op1=ALU.max,
            )
            for i in range(NS - 1):
                nc.vector.scalar_tensor_tensor(
                    out=gate_tile("below%d" % i)[:], in0=gate["diff%d" % i][:],
                    scalar=diff_bias[:, i : i + 1], in1=gate["top"][:], op0=ALU.add, op1=ALU.subtract,
                )

        def exponentials(b):
            for i in range(NS - 1):
                nc.scalar.activation(
                    out=gate_tile("expo%d" % i)[:], in_=gate["below%d" % i][:], func=ACT.Exp
                )
            nc.scalar.activation(
                out=gate_tile("expo%d" % (NS - 1))[:], in_=gate["top"][:], func=ACT.Exp, scale=-1.0
            )
            for s in range(NS):
                if s < NS - 1:
                    gate["y%d" % s] = psum_mx.tile([P, BLOCK], F32, name="y%d" % s, tag="mx%d" % s)
                else:
                    gate["y%d" % s] = psum_sn.tile([P, BLOCK], F32, name="y%d" % s, tag="numer")
                product(gate["y%d" % s], b, PASSES_OF_STREAM[s], (0,))

        def weigh():
            for s in range(NS):
                nc.vector.scalar_tensor_tensor(
                    out=gate_tile("weighted%d" % s)[:], in0=gate["y%d" % s][:],
                    scalar=param[:, OUT_BIAS_ROW + s : OUT_BIAS_ROW + s + 1],
                    in1=gate["expo%d" % s][:], op0=ALU.add, op1=ALU.mult,
                )

        def denominator():
            gate["denom"] = psum_sn.tile([P, BLOCK], F32, name="denom")
            sum_transposed(gate["denom"], [gate["expo%d" % i] for i in range(NS)])

        def numerator():
            gate["numer"] = psum_sn.tile([P, BLOCK], F32, name="numer", tag="numer")
            sum_transposed(gate["numer"], [gate["weighted%d" % s] for s in range(NS)])
            nc.scalar.activation(out=gate_tile("log_denom")[:], in_=gate["denom"][:], func=ACT.Ln)

        def invert():
            nc.scalar.activation(
                out=gate_tile("inverse")[:], in_=gate["log_denom"][:], func=ACT.Exp, scale=-1.0
            )

        def finish(b):
            merged = out_pool.tile([P, BLOCK], F32)
            nc.vector.tensor_mul(out=merged[:], in0=gate["numer"][:], in1=gate["inverse"][:])
            nc.sync.dma_start(
                out=out[b * BLOCK : (b + 1) * BLOCK, :].rearrange("(p t) n -> p (t n)", t=ROW_TILES),
                in_=merged[:],
            )

        def step(n):
            def at(lag):
                if 0 <= n - lag < N_BLOCKS * STEPS_PER_BLOCK:
                    return divmod(n - lag, STEPS_PER_BLOCK)
                return None

            merging = at(MERGE_LAG)
            if merging and merging[1] == 0:
                logit_difference(merging[0], 0)
            if merging and merging[1] == 1:
                take_off_maximum()
            if merging and merging[1] == 2:
                weigh()
                denominator()
            if merging and merging[1] == 3:
                invert()
            if at(RSTD_LAG) and at(RSTD_LAG)[1] == 0:
                rstd_of(at(RSTD_LAG)[0])
            if at(NORM_LAG):
                normalise(*at(NORM_LAG))
            if at(TRANSPOSE_LAG):
                transpose_and_scale(*at(TRANSPOSE_LAG))
            if at(QUANT_LAG):
                quantise_features(*at(QUANT_LAG))
            if at(0):
                b, g = at(0)
                statistics(b, g)
                if g == 0 and b + 1 < N_BLOCKS:
                    load(b + 1)
            if at(REGROUP_LAG):
                regroup_features(*at(REGROUP_LAG))
            if merging and merging[1] == 0:
                logit_difference(merging[0], 1)
                maximum_with_zero()
            if merging and merging[1] == 1:
                exponentials(merging[0])
            if merging and merging[1] == 2:
                numerator()
            if at(LOG_LAG) and at(LOG_LAG)[1] == 0:
                log_variance(at(LOG_LAG)[0])
            if at(RSTD_LAG) and at(RSTD_LAG)[1] == 0:
                shift_of(at(RSTD_LAG)[0])
            if merging and merging[1] == 3:
                finish(merging[0])

        load(0)
        load_small_vectors()
        load_weights()
        for n in range(REGROUP_LAG):
            step(n)
        quantise_weights()
        for n in range(REGROUP_LAG, N_STEPS):
            step(n)
